import numpy as np
import ml_dtypes


def mxq(x, axis, fmt="e4m3"):
    dtype, down = {"e4m3": (ml_dtypes.float8_e4m3fn, 7), "e5m2": (ml_dtypes.float8_e5m2, 14)}[fmt]
    v = np.moveaxis(np.asarray(x, np.float32).astype(ml_dtypes.bfloat16).astype(np.float64), axis, -1)
    blocks = v.reshape(v.shape[:-1] + (-1, 32))
    amax = np.abs(blocks).max(-1, keepdims=True)
    byte = np.maximum(np.where(amax > 0, np.frexp(amax)[1] - 1 + 127, 0) - down, 1)
    scale = np.exp2(byte - 127.0)
    codes = (blocks / scale).astype(np.float32).astype(dtype).astype(np.float64)
    return np.moveaxis((codes * scale).reshape(v.shape), -1, axis)


WIDE = False


def mx_kscale(k):
    if not WIDE:
        return np.ones(k)
    levels = np.array([10, -10, 5, -5, 0])
    a = np.random.permutation(np.resize(levels, k // 512 * 4)).reshape(k // 512, 4)
    idx = np.arange(k)
    return np.exp2(a[idx // 512, idx % 128 // 32])


BF16 = ml_dtypes.bfloat16


def bf(x):
    return np.asarray(x, np.float32).astype(BF16)


def f64(x):
    return np.asarray(x).astype(np.float64)


E2M1 = np.array([0.0, 0.5, 1.0, 1.5, 2.0, 3.0, 4.0, 6.0, -0.0, -0.5, -1.0, -1.5, -2.0, -3.0, -4.0, -6.0])


def pack_weight(w, fmt):
    k, n = w.shape
    w = f64(bf(w)).reshape(k // 32, 32, n)
    amax = np.abs(w).max(1)
    if fmt == "e4m3":
        byte = np.frexp(amax)[1] - 1 + 127 - 7
    else:
        mant, ex = np.frexp(amax / 6.0)
        byte = np.where(mant > 0.5, ex, ex - 1) + 127
    byte = np.clip(np.where(amax > 0, byte, 1), 1, 254)
    scaled = (w * np.exp2(127.0 - byte)[:, None, :]).reshape(k, n).astype(np.float32)
    by_word = np.ascontiguousarray(scaled.reshape(k // 512, 128, 4, n).transpose(0, 1, 3, 2))
    if fmt == "e4m3":
        words = by_word.astype(ml_dtypes.float8_e4m3fn).view(np.uint8)
    else:
        c = by_word.astype(ml_dtypes.float4_e2m1fn).view(np.uint8) & 0xF
        words = c[..., 0::2] | (c[..., 1::2] << 4)
    return np.ascontiguousarray(words), np.ascontiguousarray(byte.astype(np.uint8).reshape(k // 512, 16, n))


def unpack_weight(words, scales, fmt):
    g, p, n, _ = words.shape
    if fmt == "e4m3":
        vals = np.ascontiguousarray(words).view(ml_dtypes.float8_e4m3fn).astype(np.float64)
    else:
        nib = np.empty((g, p, n, 4), np.uint8)
        nib[..., 0::2] = words & 0xF
        nib[..., 1::2] = words >> 4
        vals = E2M1[nib]
    vals = vals * np.repeat(np.exp2(scales.astype(np.float64) - 127.0), 8, axis=1)[..., None]
    return vals.transpose(0, 1, 3, 2).reshape(g * 512, n)


B, IN_F, OUT_F, N_ACT = 128, 4096, 4096, 4
FMT = "e4m3"


def sigmoid(v):
    return 1.0 / (1.0 + np.exp(-v))


def setup_inputs():
    s = mx_kscale(IN_F)
    limit = np.sqrt(6.0 / (IN_F + OUT_F))
    x = bf(np.random.standard_normal((B, IN_F)) * s)
    w = np.random.uniform(-limit, limit, (OUT_F, IN_F)) / s[None, :]
    words, scales = pack_weight(np.ascontiguousarray(w.T), FMT)
    b = bf(np.random.standard_normal(OUT_F) * 0.1)
    return {"input": x,
            "W_words": words,
            "W_scales": scales,
            "b": b}


def _apply_cyclic_acts(y):
    Bb, O = y.shape
    yg = y.reshape(Bb, O // N_ACT, N_ACT)
    out = np.stack([
        np.tanh(yg[..., 0]),
        np.sin(yg[..., 1]),
        np.maximum(yg[..., 2], 0.0),
        sigmoid(yg[..., 3]),
    ], axis=-1)
    return out.reshape(Bb, O)


def reference(input, W_words, W_scales, b):
    y = (mxq(f64(input), 1, "e4m3") @ unpack_weight(W_words, W_scales, FMT)) + f64(b)
    return _apply_cyclic_acts(y)

@@ -1,0 +1,190 @@
+import math
+from contextlib import ExitStack
+
+import concourse.mybir as mybir
+from concourse.masks import make_identity
+
+FLOPS = 2 * 128 * 4096 * 4096
+
+F32 = mybir.dt.float32
+BF16 = mybir.dt.bfloat16
+I32 = mybir.dt.int32
+U32 = mybir.dt.uint32
+U8 = mybir.dt.uint8
+FP8X4 = mybir.dt.float8_e4m3fn_x4
+ALU = mybir.AluOpType
+ACT = mybir.ActivationFunctionType
+
+P = 128
+GROUPS = 8
+BANK = 512
+QUARTER = BANK // 4
+BATCHES = ((0, 4), (4, 6), (6, 7), (7, 8))
+TANH, SIN, RELU, SIGMOID = 0, 1, 2, 3
+PI_HI = 3.140625
+PI_LO = math.pi - PI_HI
+
+
+def tile_vdl_w_kernel(tc, x, w_words, w_scales, b, out):
+    nc = tc.nc
+    with ExitStack() as ctx:
+        keep = ctx.enter_context(tc.tile_pool(name="keep", bufs=1))
+        psum = ctx.enter_context(tc.psum_pool(name="psum", bufs=1))
+        ctx.enter_context(tc.manual_schedule())
+
+        bias_rows = keep.tile([P, BANK], BF16, name="bias_rows")
+        nc.vector.memset(bias_rows[:].bitcast(I32), 0)
+        planes = [keep.tile([P, 4096], U8, name="plane%d" % h, align_bytes=64) for h in range(2)]
+        for h in range(2):
+            nc.vector.memset(planes[h][:].bitcast(I32), 0)
+        warm_in = keep.tile([P, 1], F32, name="warm_in")
+        warm_out = keep.tile([P, 1], F32, name="warm_out")
+        nc.vector.memset(warm_in[:], 0.0)
+        ident_f = keep.tile([P, P], F32, name="ident_f")
+        ident_b = keep.tile([P, P], BF16, name="ident_b")
+        make_identity(nc, ident_f[:])
+        make_identity(nc, ident_b[:])
+
+        def load_table(func):
+            nc.scalar.activation(out=warm_out[:], in_=warm_in[:], func=func)
+
+        load_table(ACT.Sigmoid)
+
+        x_sb = keep.tile([P, 4096], BF16, name="x_sb")
+        nc.sync.dma_start(out=x_sb[:], in_=x[:, :])
+        nc.sync.dma_start(out=bias_rows[0:8, :], in_=b.rearrange("(j n) -> j n", j=8))
+        for h in range(2):
+            for q in range(4):
+                nc.sync.dma_start(
+                    out=planes[h][32 * q : 32 * q + 16, :].bitcast(I32),
+                    in_=w_scales[4 * h : 4 * h + 4, 4 * q : 4 * q + 4, :].bitcast(I32),
+                )
+        w_sb = {}
+        for bi, (j0, j1) in enumerate(BATCHES):
+            for g in range(GROUPS):
+                wt = keep.tile([P, BANK * (j1 - j0)], U32, name="w%d_%d" % (bi, g), align_bytes=64)
+                nc.sync.dma_start(
+                    out=wt[:].bitcast(I32),
+                    in_=w_words[g].rearrange("p n t -> p (n t)")[:, 4 * BANK * j0 : 4 * BANK * j1].bitcast(I32),
+                )
+                w_sb[(bi, g)] = wt
+
+        x_words = x_sb[:].bitcast(F32)
+        x_t = []
+        for t in range(4):
+            xt = psum.tile([P, 2, 2, P], F32, name="xt%d" % t, tag="bank%d" % t)
+            for gi in range(2):
+                g = 2 * t + gi
+                for u in range(2):
+                    nc.tensor.transpose(xt[:, gi, u, :], x_words[:, 256 * g + u : 256 * (g + 1) : 2], ident_f[:])
+            x_t.append(xt)
+        grouped = []
+        for t in range(4):
+            gt = keep.tile([P, 2, P, 4], BF16, name="grouped%d" % t, align_bytes=64)
+            src = x_t[t][:].rearrange("p g u r -> p g r u")
+            if t % 2 == 0:
+                nc.vector.tensor_copy(out=gt[:].bitcast(F32), in_=src)
+            else:
+                nc.scalar.copy(out=gt[:].bitcast(F32), in_=src)
+            grouped.append(gt)
+        x_codes = []
+        x_scales = []
+        for t in range(4):
+            xc = keep.tile([P, 2 * P], U32, name="x_codes%d" % t, align_bytes=64)
+            xs = keep.tile([P, 2 * P], U8, name="x_scales%d" % t, align_bytes=64)
+            nc.vector.quantize_mx(
+                out=xc[:].bitcast(FP8X4),
+                scales=xs[:],
+                in_=grouped[t][:].rearrange("p g r t -> p (g r t)"),
+            )
+            x_codes.append(xc)
+            x_scales.append(xs)
+
+        bias_p = keep.tile([P, 4, 8 * QUARTER], F32, name="bias_p")
+
+        def bias_round(r):
+            spread = []
+            for i in range(4):
+                bp = psum.tile([P, BANK], F32, name="bp%d_%d" % (r, i), tag="bank%d" % (4 + i))
+                j = 4 * r + i
+                nc.tensor.matmul(
+                    out=bp[:],
+                    lhsT=ident_b[:, j : j + 1].to_broadcast([P, P]),
+                    rhs=bias_rows[:],
+                    start=True,
+                    stop=True,
+                )
+                spread.append(bp)
+            for i in range(4):
+                j = 4 * r + i
+                dst = bias_p[:, :, QUARTER * j : QUARTER * (j + 1)]
+                src = spread[i][:].rearrange("p (c a) -> p a c", a=4)
+                if i % 2 == 0:
+                    nc.scalar.copy(out=dst, in_=src)
+                else:
+                    nc.vector.tensor_copy(out=dst, in_=src)
+
+        acc = {}
+
+        def passes(bi, g):
+            j0, j1 = BATCHES[bi]
+            for j in range(j0, j1):
+                if g == 0:
+                    acc[j] = psum.tile([P, BANK], F32, name="acc%d" % j, tag="bank%d" % j)
+                k = 4 * (g % 4)
+                nc.tensor.matmul_mx(
+                    out=acc[j][:],
+                    lhsT=x_codes[g // 2][:, P * (g % 2) : P * (g % 2 + 1)].bitcast(FP8X4),
+                    lhsT_scale=x_scales[g // 2][:, P * (g % 2) : P * (g % 2 + 1)],
+                    rhs=w_sb[(bi, g)][:, BANK * (j - j0) : BANK * (j - j0 + 1)].bitcast(FP8X4),
+                    rhs_scale=planes[g // 4][k:P, BANK * j : BANK * (j + 1)],
+                    start=(g == 0),
+                    stop=(g == GROUPS - 1),
+                )
+
+        def epilogue(bi):
+            j0, j1 = BATCHES[bi]
+            width = QUARTER * (j1 - j0)
+            y = keep.tile([P, 4, width], F32, name="y%d" % bi)
+            turns_i = keep.tile([P, width], I32, name="turns_i%d" % bi)
+            turns_f = keep.tile([P, width], F32, name="turns_f%d" % bi)
+            res = keep.tile([P, 4 * width], F32, name="res%d" % bi)
+            for j in range(j0, j1):
+                nc.vector.tensor_tensor(
+                    out=y[:, :, QUARTER * (j - j0) : QUARTER * (j - j0 + 1)],
+                    in0=acc[j][:].rearrange("p (c a) -> p a c", a=4),
+                    in1=bias_p[:, :, QUARTER * j : QUARTER * (j + 1)],
+                    op=ALU.add,
+                )
+            nc.scalar.activation(out=y[:, SIGMOID, :], in_=y[:, SIGMOID, :], func=ACT.Sigmoid)
+            nc.scalar.activation(out=y[:, TANH, :], in_=y[:, TANH, :], func=ACT.Tanh)
+            load_table(ACT.Sin)
+            v = y[:, SIN, :]
+            nc.vector.tensor_scalar(out=turns_i[:], in0=v, scalar1=1.0 / math.pi, scalar2=None, op0=ALU.mult)
+            nc.vector.tensor_copy(out=turns_f[:], in_=turns_i[:])
+            nc.vector.scalar_tensor_tensor(out=v, in0=turns_f[:], scalar=-PI_HI, in1=v, op0=ALU.mult, op1=ALU.add)
+            nc.vector.scalar_tensor_tensor(out=v, in0=turns_f[:], scalar=-PI_LO, in1=v, op0=ALU.mult, op1=ALU.add)
+            nc.vector.tensor_scalar(out=turns_i[:], in0=turns_i[:], scalar1=1, scalar2=None, op0=ALU.bitwise_and)
+            nc.vector.tensor_scalar(
+                out=turns_f[:], in0=turns_i[:], scalar1=-2.0, scalar2=1.0, op0=ALU.mult, op1=ALU.add
+            )
+            nc.vector.tensor_tensor(out=v, in0=v, in1=turns_f[:], op=ALU.mult)
+            nc.vector.tensor_scalar_max(out=y[:, RELU, :], in0=y[:, RELU, :], scalar1=0.0)
+            nc.scalar.activation(out=v, in_=v, func=ACT.Sin)
+            if bi + 1 < len(BATCHES):
+                load_table(ACT.Sigmoid)
+            nc.vector.tensor_copy(
+                out=res[:].rearrange("p (c a) -> p c a", a=4), in_=y[:].rearrange("p a c -> p c a")
+            )
+            nc.sync.dma_start(out=out[:, BANK * j0 : BANK * j1], in_=res[:])
+
+        bias_round(0)
+        passes(0, 0)
+        bias_round(1)
+        for g in range(1, GROUPS):
+            passes(0, g)
+        epilogue(0)
+        for bi in range(1, len(BATCHES)):
+            for g in range(GROUPS):
+                passes(bi, g)
+            epilogue(bi)

@@ -55,9 +55,9 @@ def tile_vdl_w_kernel(tc, x, w_words, w_scales, b, out):
         nc.sync.dma_start(out=bias_rows[0:8, :], in_=b.rearrange("(j n) -> j n", j=8))
         for h in range(2):
             for q in range(4):
-                nc.sync.dma_start(
-                    out=planes[h][32 * q : 32 * q + 16, :].bitcast(I32),
-                    in_=w_scales[4 * h : 4 * h + 4, 4 * q : 4 * q + 4, :].bitcast(I32),
+                nc.gpsimd.dma_start(
+                    out=planes[h][32 * q : 32 * q + 16, :].bitcast(F32),
+                    in_=w_scales[4 * h : 4 * h + 4, 4 * q : 4 * q + 4, :].bitcast(F32),
                 )
         w_sb = {}
         for bi, (j0, j1) in enumerate(BATCHES):

@@ -32,11 +32,11 @@ def tile_vdl_w_kernel(tc, x, w_words, w_scales, b, out):
         psum = ctx.enter_context(tc.psum_pool(name="psum", bufs=1))
         ctx.enter_context(tc.manual_schedule())
 
-        bias_rows = keep.tile([P, BANK], BF16, name="bias_rows")
-        nc.vector.memset(bias_rows[:].bitcast(I32), 0)
         planes = [keep.tile([P, 4096], U8, name="plane%d" % h, align_bytes=64) for h in range(2)]
         for h in range(2):
             nc.vector.memset(planes[h][:].bitcast(I32), 0)
+        bias_rows = keep.tile([P, BANK], BF16, name="bias_rows")
+        nc.vector.memset(bias_rows[:].bitcast(I32), 0)
         warm_in = keep.tile([P, 1], F32, name="warm_in")
         warm_out = keep.tile([P, 1], F32, name="warm_out")
         nc.vector.memset(warm_in[:], 0.0)
@@ -55,9 +55,9 @@ def tile_vdl_w_kernel(tc, x, w_words, w_scales, b, out):
         nc.sync.dma_start(out=bias_rows[0:8, :], in_=b.rearrange("(j n) -> j n", j=8))
         for h in range(2):
             for q in range(4):
-                nc.gpsimd.dma_start(
-                    out=planes[h][32 * q : 32 * q + 16, :].bitcast(F32),
-                    in_=w_scales[4 * h : 4 * h + 4, 4 * q : 4 * q + 4, :].bitcast(F32),
+                nc.sync.dma_start(
+                    out=planes[h][32 * q : 32 * q + 16, :].bitcast(I32),
+                    in_=w_scales[4 * h : 4 * h + 4, 4 * q : 4 * q + 4, :].bitcast(I32),
                 )
         w_sb = {}
         for bi, (j0, j1) in enumerate(BATCHES):
@@ -142,49 +142,101 @@ def tile_vdl_w_kernel(tc, x, w_words, w_scales, b, out):
                     stop=(g == GROUPS - 1),
                 )
 
-        def epilogue(bi):
-            j0, j1 = BATCHES[bi]
-            width = QUARTER * (j1 - j0)
-            y = keep.tile([P, 4, width], F32, name="y%d" % bi)
-            turns_i = keep.tile([P, width], I32, name="turns_i%d" % bi)
-            turns_f = keep.tile([P, width], F32, name="turns_f%d" % bi)
-            res = keep.tile([P, 4 * width], F32, name="res%d" % bi)
-            for j in range(j0, j1):
-                nc.vector.tensor_tensor(
-                    out=y[:, :, QUARTER * (j - j0) : QUARTER * (j - j0 + 1)],
-                    in0=acc[j][:].rearrange("p (c a) -> p a c", a=4),
-                    in1=bias_p[:, :, QUARTER * j : QUARTER * (j + 1)],
-                    op=ALU.add,
-                )
-            nc.scalar.activation(out=y[:, SIGMOID, :], in_=y[:, SIGMOID, :], func=ACT.Sigmoid)
-            nc.scalar.activation(out=y[:, TANH, :], in_=y[:, TANH, :], func=ACT.Tanh)
-            load_table(ACT.Sin)
-            v = y[:, SIN, :]
-            nc.vector.tensor_scalar(out=turns_i[:], in0=v, scalar1=1.0 / math.pi, scalar2=None, op0=ALU.mult)
-            nc.vector.tensor_copy(out=turns_f[:], in_=turns_i[:])
-            nc.vector.scalar_tensor_tensor(out=v, in0=turns_f[:], scalar=-PI_HI, in1=v, op0=ALU.mult, op1=ALU.add)
-            nc.vector.scalar_tensor_tensor(out=v, in0=turns_f[:], scalar=-PI_LO, in1=v, op0=ALU.mult, op1=ALU.add)
-            nc.vector.tensor_scalar(out=turns_i[:], in0=turns_i[:], scalar1=1, scalar2=None, op0=ALU.bitwise_and)
-            nc.vector.tensor_scalar(
-                out=turns_f[:], in0=turns_i[:], scalar1=-2.0, scalar2=1.0, op0=ALU.mult, op1=ALU.add
-            )
-            nc.vector.tensor_tensor(out=v, in0=v, in1=turns_f[:], op=ALU.mult)
-            nc.vector.tensor_scalar_max(out=y[:, RELU, :], in0=y[:, RELU, :], scalar1=0.0)
-            nc.scalar.activation(out=v, in_=v, func=ACT.Sin)
-            if bi + 1 < len(BATCHES):
-                load_table(ACT.Sigmoid)
-            nc.vector.tensor_copy(
-                out=res[:].rearrange("p (c a) -> p c a", a=4), in_=y[:].rearrange("p a c -> p c a")
-            )
-            nc.sync.dma_start(out=out[:, BANK * j0 : BANK * j1], in_=res[:])
-
         bias_round(0)
         passes(0, 0)
         bias_round(1)
         for g in range(1, GROUPS):
             passes(0, g)
-        epilogue(0)
         for bi in range(1, len(BATCHES)):
             for g in range(GROUPS):
                 passes(bi, g)
-            epilogue(bi)
+
+        y = []
+        turns_i = []
+        turns_f = []
+        sign_f = []
+        res = []
+        for bi, (j0, j1) in enumerate(BATCHES):
+            width = QUARTER * (j1 - j0)
+            y.append(keep.tile([P, 4, width], F32, name="y%d" % bi))
+            turns_i.append(keep.tile([P, width], I32, name="turns_i%d" % bi))
+            turns_f.append(keep.tile([P, width], F32, name="turns_f%d" % bi))
+            sign_f.append(keep.tile([P, width], F32, name="sign_f%d" % bi))
+            res.append(keep.tile([P, 4 * width], F32, name="res%d" % bi))
+
+        def add_bias(bi, j, planes_of):
+            j0 = BATCHES[bi][0]
+            nc.vector.tensor_tensor(
+                out=y[bi][:, planes_of, QUARTER * (j - j0) : QUARTER * (j - j0 + 1)],
+                in0=acc[j][:].rearrange("p (c a) -> p a c", a=4)[:, planes_of, :],
+                in1=bias_p[:, planes_of, QUARTER * j : QUARTER * (j + 1)],
+                op=ALU.add,
+            )
+
+        def add_bias_all(bi):
+            for j in range(BATCHES[bi][0], BATCHES[bi][1]):
+                add_bias(bi, j, slice(0, 4))
+
+        def sigmoid_tanh(bi):
+            nc.scalar.activation(out=y[bi][:, SIGMOID, :], in_=y[bi][:, SIGMOID, :], func=ACT.Sigmoid)
+            nc.scalar.activation(out=y[bi][:, TANH, :], in_=y[bi][:, TANH, :], func=ACT.Tanh)
+
+        def fold(bi):
+            v = y[bi][:, SIN, :]
+            ki = turns_i[bi][:]
+            kf = turns_f[bi][:]
+            sg = sign_f[bi][:]
+            nc.vector.tensor_scalar(out=ki, in0=v, scalar1=1.0 / math.pi, scalar2=None, op0=ALU.mult)
+            nc.vector.tensor_copy(out=kf, in_=ki)
+            nc.vector.tensor_scalar(out=ki, in0=ki, scalar1=1, scalar2=None, op0=ALU.bitwise_and)
+            nc.vector.scalar_tensor_tensor(out=v, in0=kf, scalar=-PI_HI, in1=v, op0=ALU.mult, op1=ALU.add)
+            nc.vector.tensor_scalar(out=sg, in0=ki, scalar1=-2.0, scalar2=1.0, op0=ALU.mult, op1=ALU.add)
+            nc.vector.scalar_tensor_tensor(out=v, in0=kf, scalar=-PI_LO, in1=v, op0=ALU.mult, op1=ALU.add)
+            nc.vector.tensor_tensor(out=v, in0=v, in1=sg, op=ALU.mult)
+
+        def relu(bi):
+            nc.vector.tensor_scalar_max(out=y[bi][:, RELU, :], in0=y[bi][:, RELU, :], scalar1=0.0)
+
+        def sine(bi):
+            nc.scalar.activation(out=y[bi][:, SIN, :], in_=y[bi][:, SIN, :], func=ACT.Sin)
+
+        def finish(bi):
+            j0, j1 = BATCHES[bi]
+            nc.vector.tensor_copy(
+                out=res[bi][:].rearrange("p (c a) -> p c a", a=4), in_=y[bi][:].rearrange("p a c -> p c a")
+            )
+            nc.sync.dma_start(out=out[:, BANK * j0 : BANK * j1], in_=res[bi][:])
+
+        add_bias_all(0)
+        sigmoid_tanh(0)
+        load_table(ACT.Sin)
+        fold(0)
+        relu(0)
+        sine(0)
+        load_table(ACT.Sigmoid)
+        finish(0)
+
+        add_bias_all(1)
+        sigmoid_tanh(1)
+        load_table(ACT.Sin)
+        fold(1)
+        relu(1)
+        sine(1)
+
+        add_bias_all(2)
+        fold(2)
+        relu(2)
+        sine(2)
+        load_table(ACT.Sigmoid)
+        sigmoid_tanh(2)
+        finish(1)
+
+        add_bias(3, 7, slice(0, 4, 3))
+        add_bias(3, 7, slice(1, 3))
+        sigmoid_tanh(3)
+        load_table(ACT.Sin)
+        fold(3)
+        finish(2)
+        relu(3)
+        sine(3)
+        finish(3)

@@ -43,6 +43,12 @@ def tile_vdl_w_kernel(tc, x, w_words, w_scales, b, out):
         ident_f = keep.tile([P, P], F32, name="ident_f")
         ident_b = keep.tile([P, P], BF16, name="ident_b")
         make_identity(nc, ident_f[:])
+        for h in range(2):
+            for q in range(4):
+                nc.gpsimd.dma_start(
+                    out=planes[h][32 * q : 32 * q + 16, :].bitcast(F32),
+                    in_=w_scales[4 * h : 4 * h + 4, 4 * q : 4 * q + 4, :].bitcast(F32),
+                )
         make_identity(nc, ident_b[:])
 
         def load_table(func):
@@ -53,12 +59,6 @@ def tile_vdl_w_kernel(tc, x, w_words, w_scales, b, out):
         x_sb = keep.tile([P, 4096], BF16, name="x_sb")
         nc.sync.dma_start(out=x_sb[:], in_=x[:, :])
         nc.sync.dma_start(out=bias_rows[0:8, :], in_=b.rearrange("(j n) -> j n", j=8))
-        for h in range(2):
-            for q in range(4):
-                nc.sync.dma_start(
-                    out=planes[h][32 * q : 32 * q + 16, :].bitcast(I32),
-                    in_=w_scales[4 * h : 4 * h + 4, 4 * q : 4 * q + 4, :].bitcast(I32),
-                )
         w_sb = {}
         for bi, (j0, j1) in enumerate(BATCHES):
             for g in range(GROUPS):

@@ -43,12 +43,11 @@ def tile_vdl_w_kernel(tc, x, w_words, w_scales, b, out):
         ident_f = keep.tile([P, P], F32, name="ident_f")
         ident_b = keep.tile([P, P], BF16, name="ident_b")
         make_identity(nc, ident_f[:])
-        for h in range(2):
-            for q in range(4):
-                nc.gpsimd.dma_start(
-                    out=planes[h][32 * q : 32 * q + 16, :].bitcast(F32),
-                    in_=w_scales[4 * h : 4 * h + 4, 4 * q : 4 * q + 4, :].bitcast(F32),
-                )
+        for q in range(4):
+            nc.gpsimd.dma_start(
+                out=planes[1][32 * q : 32 * q + 16, :].bitcast(F32),
+                in_=w_scales[4:8, 4 * q : 4 * q + 4, :].bitcast(F32),
+            )
         make_identity(nc, ident_b[:])
 
         def load_table(func):
@@ -59,6 +58,11 @@ def tile_vdl_w_kernel(tc, x, w_words, w_scales, b, out):
         x_sb = keep.tile([P, 4096], BF16, name="x_sb")
         nc.sync.dma_start(out=x_sb[:], in_=x[:, :])
         nc.sync.dma_start(out=bias_rows[0:8, :], in_=b.rearrange("(j n) -> j n", j=8))
+        for q in range(4):
+            nc.sync.dma_start(
+                out=planes[0][32 * q : 32 * q + 16, :].bitcast(I32),
+                in_=w_scales[0:4, 4 * q : 4 * q + 4, :].bitcast(I32),
+            )
         w_sb = {}
         for bi, (j0, j1) in enumerate(BATCHES):
             for g in range(GROUPS):

@@ -37,32 +37,20 @@ def tile_vdl_w_kernel(tc, x, w_words, w_scales, b, out):
             nc.vector.memset(planes[h][:].bitcast(I32), 0)
         bias_rows = keep.tile([P, BANK], BF16, name="bias_rows")
         nc.vector.memset(bias_rows[:].bitcast(I32), 0)
-        warm_in = keep.tile([P, 1], F32, name="warm_in")
-        warm_out = keep.tile([P, 1], F32, name="warm_out")
-        nc.vector.memset(warm_in[:], 0.0)
         ident_f = keep.tile([P, P], F32, name="ident_f")
         ident_b = keep.tile([P, P], BF16, name="ident_b")
         make_identity(nc, ident_f[:])
-        for q in range(4):
-            nc.gpsimd.dma_start(
-                out=planes[1][32 * q : 32 * q + 16, :].bitcast(F32),
-                in_=w_scales[4:8, 4 * q : 4 * q + 4, :].bitcast(F32),
-            )
+        for h in range(2):
+            for q in range(4):
+                nc.gpsimd.dma_start(
+                    out=planes[h][32 * q : 32 * q + 16, :].bitcast(F32),
+                    in_=w_scales[4 * h : 4 * h + 4, 4 * q : 4 * q + 4, :].bitcast(F32),
+                )
         make_identity(nc, ident_b[:])
-
-        def load_table(func):
-            nc.scalar.activation(out=warm_out[:], in_=warm_in[:], func=func)
-
-        load_table(ACT.Sigmoid)
 
         x_sb = keep.tile([P, 4096], BF16, name="x_sb")
         nc.sync.dma_start(out=x_sb[:], in_=x[:, :])
         nc.sync.dma_start(out=bias_rows[0:8, :], in_=b.rearrange("(j n) -> j n", j=8))
-        for q in range(4):
-            nc.sync.dma_start(
-                out=planes[0][32 * q : 32 * q + 16, :].bitcast(I32),
-                in_=w_scales[0:4, 4 * q : 4 * q + 4, :].bitcast(I32),
-            )
         w_sb = {}
         for bi, (j0, j1) in enumerate(BATCHES):
             for g in range(GROUPS):
@@ -213,16 +201,13 @@ def tile_vdl_w_kernel(tc, x, w_words, w_scales, b, out):
 
         add_bias_all(0)
         sigmoid_tanh(0)
-        load_table(ACT.Sin)
         fold(0)
         relu(0)
         sine(0)
-        load_table(ACT.Sigmoid)
         finish(0)
 
         add_bias_all(1)
         sigmoid_tanh(1)
-        load_table(ACT.Sin)
         fold(1)
         relu(1)
         sine(1)
@@ -231,14 +216,12 @@ def tile_vdl_w_kernel(tc, x, w_words, w_scales, b, out):
         fold(2)
         relu(2)
         sine(2)
-        load_table(ACT.Sigmoid)
         sigmoid_tanh(2)
         finish(1)
 
         add_bias(3, 7, slice(0, 4, 3))
         add_bias(3, 7, slice(1, 3))
         sigmoid_tanh(3)
-        load_table(ACT.Sin)
         fold(3)
         finish(2)
         relu(3)

@@ -32,6 +32,10 @@ def tile_vdl_w_kernel(tc, x, w_words, w_scales, b, out):
         psum = ctx.enter_context(tc.psum_pool(name="psum", bufs=1))
         ctx.enter_context(tc.manual_schedule())
 
+        warm = keep.tile([P, 2], F32, name="warm")
+        nc.vector.memset(warm[:, 0:1], 0.0)
+        nc.scalar.activation(out=warm[:, 1:2], in_=warm[:, 0:1], func=ACT.Silu)
+
         planes = [keep.tile([P, 4096], U8, name="plane%d" % h, align_bytes=64) for h in range(2)]
         for h in range(2):
             nc.vector.memset(planes[h][:].bitcast(I32), 0)
@@ -170,8 +174,9 @@ def tile_vdl_w_kernel(tc, x, w_words, w_scales, b, out):
                 add_bias(bi, j, slice(0, 4))
 
         def sigmoid_tanh(bi):
-            nc.scalar.activation(out=y[bi][:, SIGMOID, :], in_=y[bi][:, SIGMOID, :], func=ACT.Sigmoid)
+            nc.scalar.activation(out=y[bi][:, SIGMOID, :], in_=y[bi][:, SIGMOID, :], func=ACT.Tanh, scale=0.5)
             nc.scalar.activation(out=y[bi][:, TANH, :], in_=y[bi][:, TANH, :], func=ACT.Tanh)
+            nc.scalar.activation(out=y[bi][:, SIGMOID, :], in_=y[bi][:, SIGMOID, :], func=ACT.Copy, scale=0.5, bias=0.5)
 
         def fold(bi):
             v = y[bi][:, SIN, :]

@@ -21,8 +21,7 @@ BANK = 512
 QUARTER = BANK // 4
 BATCHES = ((0, 4), (4, 6), (6, 7), (7, 8))
 TANH, SIN, RELU, SIGMOID = 0, 1, 2, 3
-PI_HI = 3.140625
-PI_LO = math.pi - PI_HI
+TWO_PI = 2.0 * math.pi
 
 
 def tile_vdl_w_kernel(tc, x, w_words, w_scales, b, out):
@@ -149,15 +148,11 @@ def tile_vdl_w_kernel(tc, x, w_words, w_scales, b, out):
 
         y = []
         turns_i = []
-        turns_f = []
-        sign_f = []
         res = []
         for bi, (j0, j1) in enumerate(BATCHES):
             width = QUARTER * (j1 - j0)
             y.append(keep.tile([P, 4, width], F32, name="y%d" % bi))
             turns_i.append(keep.tile([P, width], I32, name="turns_i%d" % bi))
-            turns_f.append(keep.tile([P, width], F32, name="turns_f%d" % bi))
-            sign_f.append(keep.tile([P, width], F32, name="sign_f%d" % bi))
             res.append(keep.tile([P, 4 * width], F32, name="res%d" % bi))
 
         def add_bias(bi, j, planes_of):
@@ -181,15 +176,8 @@ def tile_vdl_w_kernel(tc, x, w_words, w_scales, b, out):
         def fold(bi):
             v = y[bi][:, SIN, :]
             ki = turns_i[bi][:]
-            kf = turns_f[bi][:]
-            sg = sign_f[bi][:]
-            nc.vector.tensor_scalar(out=ki, in0=v, scalar1=1.0 / math.pi, scalar2=None, op0=ALU.mult)
-            nc.vector.tensor_copy(out=kf, in_=ki)
-            nc.vector.tensor_scalar(out=ki, in0=ki, scalar1=1, scalar2=None, op0=ALU.bitwise_and)
-            nc.vector.scalar_tensor_tensor(out=v, in0=kf, scalar=-PI_HI, in1=v, op0=ALU.mult, op1=ALU.add)
-            nc.vector.tensor_scalar(out=sg, in0=ki, scalar1=-2.0, scalar2=1.0, op0=ALU.mult, op1=ALU.add)
-            nc.vector.scalar_tensor_tensor(out=v, in0=kf, scalar=-PI_LO, in1=v, op0=ALU.mult, op1=ALU.add)
-            nc.vector.tensor_tensor(out=v, in0=v, in1=sg, op=ALU.mult)
+            nc.vector.tensor_scalar(out=ki, in0=v, scalar1=1.0 / TWO_PI, scalar2=None, op0=ALU.mult)
+            nc.vector.scalar_tensor_tensor(out=v, in0=ki, scalar=-TWO_PI, in1=v, op0=ALU.mult, op1=ALU.add)
 
         def relu(bi):
             nc.vector.tensor_scalar_max(out=y[bi][:, RELU, :], in0=y[bi][:, RELU, :], scalar1=0.0)

@@ -18,8 +18,9 @@ ACT = mybir.ActivationFunctionType
 P = 128
 GROUPS = 8
 BANK = 512
-QUARTER = BANK // 4
-BATCHES = ((0, 4), (4, 6), (6, 7), (7, 8))
+BANKS = 8
+N_OUT = 4096
+BATCHES = ((0, 2048), (2048, 3072), (3072, 3584), (3584, 4096))
 TANH, SIN, RELU, SIGMOID = 0, 1, 2, 3
 TWO_PI = 2.0 * math.pi
 
@@ -31,15 +32,15 @@ def tile_vdl_w_kernel(tc, x, w_words, w_scales, b, out):
         psum = ctx.enter_context(tc.psum_pool(name="psum", bufs=1))
         ctx.enter_context(tc.manual_schedule())
 
+        bias_rows = keep.tile([P, BANK], BF16, name="bias_rows")
+        nc.vector.memset(bias_rows[:].bitcast(I32), 0)
+        nc.scalar.dma_start(out=bias_rows[0:8, :], in_=b.rearrange("(j n) -> j n", j=8))
         warm = keep.tile([P, 2], F32, name="warm")
         nc.vector.memset(warm[:, 0:1], 0.0)
         nc.scalar.activation(out=warm[:, 1:2], in_=warm[:, 0:1], func=ACT.Silu)
-
-        planes = [keep.tile([P, 4096], U8, name="plane%d" % h, align_bytes=64) for h in range(2)]
+        planes = [keep.tile([P, N_OUT], U8, name="plane%d" % h, align_bytes=64) for h in range(2)]
         for h in range(2):
             nc.vector.memset(planes[h][:].bitcast(I32), 0)
-        bias_rows = keep.tile([P, BANK], BF16, name="bias_rows")
-        nc.vector.memset(bias_rows[:].bitcast(I32), 0)
         ident_f = keep.tile([P, P], F32, name="ident_f")
         ident_b = keep.tile([P, P], BF16, name="ident_b")
         make_identity(nc, ident_f[:])
@@ -53,14 +54,13 @@ def tile_vdl_w_kernel(tc, x, w_words, w_scales, b, out):
 
         x_sb = keep.tile([P, 4096], BF16, name="x_sb")
         nc.sync.dma_start(out=x_sb[:], in_=x[:, :])
-        nc.sync.dma_start(out=bias_rows[0:8, :], in_=b.rearrange("(j n) -> j n", j=8))
         w_sb = {}
-        for bi, (j0, j1) in enumerate(BATCHES):
+        for bi, (c0, c1) in enumerate(BATCHES):
             for g in range(GROUPS):
-                wt = keep.tile([P, BANK * (j1 - j0)], U32, name="w%d_%d" % (bi, g), align_bytes=64)
+                wt = keep.tile([P, c1 - c0], U32, name="w%d_%d" % (bi, g), align_bytes=64)
                 nc.sync.dma_start(
                     out=wt[:].bitcast(I32),
-                    in_=w_words[g].rearrange("p n t -> p (n t)")[:, 4 * BANK * j0 : 4 * BANK * j1].bitcast(I32),
+                    in_=w_words[g].rearrange("p n t -> p (n t)")[:, 4 * c0 : 4 * c1].bitcast(I32),
                 )
                 w_sb[(bi, g)] = wt
 
@@ -95,13 +95,12 @@ def tile_vdl_w_kernel(tc, x, w_words, w_scales, b, out):
             x_codes.append(xc)
             x_scales.append(xs)
 
-        bias_p = keep.tile([P, 4, 8 * QUARTER], F32, name="bias_p")
+        bias_p = keep.tile([P, 4, N_OUT // 4], F32, name="bias_p")
 
-        def bias_round(r):
+        def bias_round(js, banks):
             spread = []
-            for i in range(4):
-                bp = psum.tile([P, BANK], F32, name="bp%d_%d" % (r, i), tag="bank%d" % (4 + i))
-                j = 4 * r + i
+            for j, bank in zip(js, banks):
+                bp = psum.tile([P, BANK], F32, name="bp%d" % j, tag="bank%d" % bank)
                 nc.tensor.matmul(
                     out=bp[:],
                     lhsT=ident_b[:, j : j + 1].to_broadcast([P, P]),
@@ -110,113 +109,74 @@ def tile_vdl_w_kernel(tc, x, w_words, w_scales, b, out):
                     stop=True,
                 )
                 spread.append(bp)
-            for i in range(4):
-                j = 4 * r + i
-                dst = bias_p[:, :, QUARTER * j : QUARTER * (j + 1)]
+            for i, j in enumerate(js):
+                dst = bias_p[:, :, (BANK // 4) * j : (BANK // 4) * (j + 1)]
                 src = spread[i][:].rearrange("p (c a) -> p a c", a=4)
                 if i % 2 == 0:
                     nc.scalar.copy(out=dst, in_=src)
                 else:
                     nc.vector.tensor_copy(out=dst, in_=src)
 
+        pieces = []
+        n_pieces = 0
+        for c0, c1 in BATCHES:
+            row = []
+            for c in range(c0, c1, BANK):
+                row.append((c, min(BANK, c1 - c), n_pieces % BANKS))
+                n_pieces += 1
+            pieces.append(row)
         acc = {}
 
         def passes(bi, g):
-            j0, j1 = BATCHES[bi]
-            for j in range(j0, j1):
+            c0 = BATCHES[bi][0]
+            for c, n, bank in pieces[bi]:
                 if g == 0:
-                    acc[j] = psum.tile([P, BANK], F32, name="acc%d" % j, tag="bank%d" % j)
+                    acc[c] = psum.tile([P, n], F32, name="acc%d" % c, tag="bank%d" % bank)
                 k = 4 * (g % 4)
                 nc.tensor.matmul_mx(
-                    out=acc[j][:],
+                    out=acc[c][:],
                     lhsT=x_codes[g // 2][:, P * (g % 2) : P * (g % 2 + 1)].bitcast(FP8X4),
                     lhsT_scale=x_scales[g // 2][:, P * (g % 2) : P * (g % 2 + 1)],
-                    rhs=w_sb[(bi, g)][:, BANK * (j - j0) : BANK * (j - j0 + 1)].bitcast(FP8X4),
-                    rhs_scale=planes[g // 4][k:P, BANK * j : BANK * (j + 1)],
+                    rhs=w_sb[(bi, g)][:, c - c0 : c - c0 + n].bitcast(FP8X4),
+                    rhs_scale=planes[g // 4][k:P, c : c + n],
                     start=(g == 0),
                     stop=(g == GROUPS - 1),
                 )
 
-        bias_round(0)
+        def epilogue(bi):
+            c0, c1 = BATCHES[bi]
+            width = (c1 - c0) // 4
+            y = keep.tile([P, 4, width], F32, name="y%d" % bi)
+            turns = keep.tile([P, width], I32, name="turns%d" % bi)
+            res = keep.tile([P, 4 * width], F32, name="res%d" % bi)
+            for c, n, bank in pieces[bi]:
+                nc.vector.tensor_tensor(
+                    out=y[:, :, (c - c0) // 4 : (c - c0 + n) // 4],
+                    in0=acc[c][:].rearrange("p (c a) -> p a c", a=4),
+                    in1=bias_p[:, :, c // 4 : (c + n) // 4],
+                    op=ALU.add,
+                )
+            nc.scalar.activation(out=y[:, SIGMOID, :], in_=y[:, SIGMOID, :], func=ACT.Tanh, scale=0.5)
+            nc.scalar.activation(out=y[:, TANH, :], in_=y[:, TANH, :], func=ACT.Tanh)
+            nc.vector.tensor_scalar(out=turns[:], in0=y[:, SIN, :], scalar1=1.0 / TWO_PI, scalar2=None, op0=ALU.mult)
+            nc.vector.tensor_scalar_max(out=y[:, RELU, :], in0=y[:, RELU, :], scalar1=0.0)
+            nc.vector.scalar_tensor_tensor(
+                out=y[:, SIN, :], in0=turns[:], scalar=-TWO_PI, in1=y[:, SIN, :], op0=ALU.mult, op1=ALU.add
+            )
+            nc.scalar.activation(out=y[:, SIN, :], in_=y[:, SIN, :], func=ACT.Sin)
+            nc.vector.tensor_scalar(
+                out=y[:, SIGMOID, :], in0=y[:, SIGMOID, :], scalar1=0.5, scalar2=0.5, op0=ALU.mult, op1=ALU.add
+            )
+            nc.vector.tensor_copy(out=res[:].rearrange("p (c a) -> p c a", a=4), in_=y[:].rearrange("p a c -> p c a"))
+            nc.sync.dma_start(out=out[:, c0:c1], in_=res[:])
+
+        bias_round((0, 1, 2, 3), (4, 5, 6, 7))
         passes(0, 0)
-        bias_round(1)
+        bias_round((4, 5, 6, 7), (4, 5, 6, 7))
         for g in range(1, GROUPS):
             passes(0, g)
+        epilogue(0)
         for bi in range(1, len(BATCHES)):
             for g in range(GROUPS):
                 passes(bi, g)
-
-        y = []
-        turns_i = []
-        res = []
-        for bi, (j0, j1) in enumerate(BATCHES):
-            width = QUARTER * (j1 - j0)
-            y.append(keep.tile([P, 4, width], F32, name="y%d" % bi))
-            turns_i.append(keep.tile([P, width], I32, name="turns_i%d" % bi))
-            res.append(keep.tile([P, 4 * width], F32, name="res%d" % bi))
-
-        def add_bias(bi, j, planes_of):
-            j0 = BATCHES[bi][0]
-            nc.vector.tensor_tensor(
-                out=y[bi][:, planes_of, QUARTER * (j - j0) : QUARTER * (j - j0 + 1)],
-                in0=acc[j][:].rearrange("p (c a) -> p a c", a=4)[:, planes_of, :],
-                in1=bias_p[:, planes_of, QUARTER * j : QUARTER * (j + 1)],
-                op=ALU.add,
-            )
-
-        def add_bias_all(bi):
-            for j in range(BATCHES[bi][0], BATCHES[bi][1]):
-                add_bias(bi, j, slice(0, 4))
-
-        def sigmoid_tanh(bi):
-            nc.scalar.activation(out=y[bi][:, SIGMOID, :], in_=y[bi][:, SIGMOID, :], func=ACT.Tanh, scale=0.5)
-            nc.scalar.activation(out=y[bi][:, TANH, :], in_=y[bi][:, TANH, :], func=ACT.Tanh)
-            nc.scalar.activation(out=y[bi][:, SIGMOID, :], in_=y[bi][:, SIGMOID, :], func=ACT.Copy, scale=0.5, bias=0.5)
-
-        def fold(bi):
-            v = y[bi][:, SIN, :]
-            ki = turns_i[bi][:]
-            nc.vector.tensor_scalar(out=ki, in0=v, scalar1=1.0 / TWO_PI, scalar2=None, op0=ALU.mult)
-            nc.vector.scalar_tensor_tensor(out=v, in0=ki, scalar=-TWO_PI, in1=v, op0=ALU.mult, op1=ALU.add)
-
-        def relu(bi):
-            nc.vector.tensor_scalar_max(out=y[bi][:, RELU, :], in0=y[bi][:, RELU, :], scalar1=0.0)
-
-        def sine(bi):
-            nc.scalar.activation(out=y[bi][:, SIN, :], in_=y[bi][:, SIN, :], func=ACT.Sin)
-
-        def finish(bi):
-            j0, j1 = BATCHES[bi]
-            nc.vector.tensor_copy(
-                out=res[bi][:].rearrange("p (c a) -> p c a", a=4), in_=y[bi][:].rearrange("p a c -> p c a")
-            )
-            nc.sync.dma_start(out=out[:, BANK * j0 : BANK * j1], in_=res[bi][:])
-
-        add_bias_all(0)
-        sigmoid_tanh(0)
-        fold(0)
-        relu(0)
-        sine(0)
-        finish(0)
-
-        add_bias_all(1)
-        sigmoid_tanh(1)
-        fold(1)
-        relu(1)
-        sine(1)
-
-        add_bias_all(2)
-        fold(2)
-        relu(2)
-        sine(2)
-        sigmoid_tanh(2)
-        finish(1)
-
-        add_bias(3, 7, slice(0, 4, 3))
-        add_bias(3, 7, slice(1, 3))
-        sigmoid_tanh(3)
-        fold(3)
-        finish(2)
-        relu(3)
-        sine(3)
-        finish(3)
+            epilogue(bi)

@@ -44,16 +44,17 @@ def tile_vdl_w_kernel(tc, x, w_words, w_scales, b, out):
         ident_f = keep.tile([P, P], F32, name="ident_f")
         ident_b = keep.tile([P, P], BF16, name="ident_b")
         make_identity(nc, ident_f[:])
-        for h in range(2):
-            for q in range(4):
-                nc.gpsimd.dma_start(
-                    out=planes[h][32 * q : 32 * q + 16, :].bitcast(F32),
-                    in_=w_scales[4 * h : 4 * h + 4, 4 * q : 4 * q + 4, :].bitcast(F32),
-                )
+
         make_identity(nc, ident_b[:])
 
         x_sb = keep.tile([P, 4096], BF16, name="x_sb")
         nc.sync.dma_start(out=x_sb[:], in_=x[:, :])
+        for h in range(2):
+            for q in range(4):
+                nc.sync.dma_start(
+                    out=planes[h][32 * q : 32 * q + 16, :].bitcast(I32),
+                    in_=w_scales[4 * h : 4 * h + 4, 4 * q : 4 * q + 4, :].bitcast(I32),
+                )
         w_sb = {}
         for bi, (c0, c1) in enumerate(BATCHES):
             for g in range(GROUPS):

@@ -20,7 +20,7 @@ GROUPS = 8
 BANK = 512
 BANKS = 8
 N_OUT = 4096
-BATCHES = ((0, 2048), (2048, 3072), (3072, 3584), (3584, 4096))
+BATCHES = ((0, 2048), (2048, 3328), (3328, 3840), (3840, 4096))
 TANH, SIN, RELU, SIGMOID = 0, 1, 2, 3
 TWO_PI = 2.0 * math.pi
 
@@ -150,15 +150,16 @@ def tile_vdl_w_kernel(tc, x, w_words, w_scales, b, out):
             y = keep.tile([P, 4, width], F32, name="y%d" % bi)
             turns = keep.tile([P, width], I32, name="turns%d" % bi)
             res = keep.tile([P, 4 * width], F32, name="res%d" % bi)
-            for c, n, bank in pieces[bi]:
-                nc.vector.tensor_tensor(
-                    out=y[:, :, (c - c0) // 4 : (c - c0 + n) // 4],
-                    in0=acc[c][:].rearrange("p (c a) -> p a c", a=4),
-                    in1=bias_p[:, :, c // 4 : (c + n) // 4],
-                    op=ALU.add,
-                )
-            nc.scalar.activation(out=y[:, SIGMOID, :], in_=y[:, SIGMOID, :], func=ACT.Tanh, scale=0.5)
+            for half in (slice(0, 2), slice(2, 4)):
+                for c, n, bank in pieces[bi]:
+                    nc.vector.tensor_tensor(
+                        out=y[:, half, (c - c0) // 4 : (c - c0 + n) // 4],
+                        in0=acc[c][:].rearrange("p (c a) -> p a c", a=4)[:, half, :],
+                        in1=bias_p[:, half, c // 4 : (c + n) // 4],
+                        op=ALU.add,
+                    )
             nc.scalar.activation(out=y[:, TANH, :], in_=y[:, TANH, :], func=ACT.Tanh)
+            nc.scalar.activation(out=y[:, SIGMOID, :], in_=y[:, SIGMOID, :], func=ACT.Tanh, scale=0.5)
             nc.vector.tensor_scalar(out=turns[:], in0=y[:, SIN, :], scalar1=1.0 / TWO_PI, scalar2=None, op0=ALU.mult)
             nc.vector.tensor_scalar_max(out=y[:, RELU, :], in0=y[:, RELU, :], scalar1=0.0)
             nc.vector.scalar_tensor_tensor(

@@ -44,17 +44,19 @@ def tile_vdl_w_kernel(tc, x, w_words, w_scales, b, out):
         ident_f = keep.tile([P, P], F32, name="ident_f")
         ident_b = keep.tile([P, P], BF16, name="ident_b")
         make_identity(nc, ident_f[:])
-
-        make_identity(nc, ident_b[:])
-
-        x_sb = keep.tile([P, 4096], BF16, name="x_sb")
-        nc.sync.dma_start(out=x_sb[:], in_=x[:, :])
         for h in range(2):
             for q in range(4):
-                nc.sync.dma_start(
-                    out=planes[h][32 * q : 32 * q + 16, :].bitcast(I32),
-                    in_=w_scales[4 * h : 4 * h + 4, 4 * q : 4 * q + 4, :].bitcast(I32),
+                nc.gpsimd.dma_start(
+                    out=planes[h][32 * q : 32 * q + 16, :].bitcast(F32),
+                    in_=w_scales[4 * h : 4 * h + 4, 4 * q : 4 * q + 4, :].bitcast(F32),
                 )
+        make_identity(nc, ident_b[:])
+
+        x_sb = []
+        for t in range(4):
+            xs_t = keep.tile([P, 1024], BF16, name="x_sb%d" % t)
+            nc.sync.dma_start(out=xs_t[:], in_=x[:, 1024 * t : 1024 * (t + 1)])
+            x_sb.append(xs_t)
         w_sb = {}
         for bi, (c0, c1) in enumerate(BATCHES):
             for g in range(GROUPS):
@@ -65,33 +67,26 @@ def tile_vdl_w_kernel(tc, x, w_words, w_scales, b, out):
                 )
                 w_sb[(bi, g)] = wt
 
-        x_words = x_sb[:].bitcast(F32)
-        x_t = []
+        x_codes = []
+        x_scales = []
         for t in range(4):
+            x_words = x_sb[t][:].bitcast(F32)
             xt = psum.tile([P, 2, 2, P], F32, name="xt%d" % t, tag="bank%d" % t)
             for gi in range(2):
-                g = 2 * t + gi
                 for u in range(2):
-                    nc.tensor.transpose(xt[:, gi, u, :], x_words[:, 256 * g + u : 256 * (g + 1) : 2], ident_f[:])
-            x_t.append(xt)
-        grouped = []
-        for t in range(4):
+                    nc.tensor.transpose(xt[:, gi, u, :], x_words[:, 256 * gi + u : 256 * (gi + 1) : 2], ident_f[:])
             gt = keep.tile([P, 2, P, 4], BF16, name="grouped%d" % t, align_bytes=64)
-            src = x_t[t][:].rearrange("p g u r -> p g r u")
+            src = xt[:].rearrange("p g u r -> p g r u")
             if t % 2 == 0:
                 nc.vector.tensor_copy(out=gt[:].bitcast(F32), in_=src)
             else:
                 nc.scalar.copy(out=gt[:].bitcast(F32), in_=src)
-            grouped.append(gt)
-        x_codes = []
-        x_scales = []
-        for t in range(4):
             xc = keep.tile([P, 2 * P], U32, name="x_codes%d" % t, align_bytes=64)
             xs = keep.tile([P, 2 * P], U8, name="x_scales%d" % t, align_bytes=64)
             nc.vector.quantize_mx(
                 out=xc[:].bitcast(FP8X4),
                 scales=xs[:],
-                in_=grouped[t][:].rearrange("p g r t -> p (g r t)"),
+                in_=gt[:].rearrange("p g r t -> p (g r t)"),
             )
             x_codes.append(xc)
             x_scales.append(xs)

@@ -32,25 +32,29 @@ def tile_vdl_w_kernel(tc, x, w_words, w_scales, b, out):
         psum = ctx.enter_context(tc.psum_pool(name="psum", bufs=1))
         ctx.enter_context(tc.manual_schedule())
 
+        planes = [keep.tile([P, N_OUT], U8, name="plane%d" % h, align_bytes=64) for h in range(2)]
         bias_rows = keep.tile([P, BANK], BF16, name="bias_rows")
         nc.vector.memset(bias_rows[:].bitcast(I32), 0)
         nc.scalar.dma_start(out=bias_rows[0:8, :], in_=b.rearrange("(j n) -> j n", j=8))
+        nc.vector.memset(planes[0][:].bitcast(I32), 0)
         warm = keep.tile([P, 2], F32, name="warm")
         nc.vector.memset(warm[:, 0:1], 0.0)
         nc.scalar.activation(out=warm[:, 1:2], in_=warm[:, 0:1], func=ACT.Silu)
-        planes = [keep.tile([P, N_OUT], U8, name="plane%d" % h, align_bytes=64) for h in range(2)]
-        for h in range(2):
-            nc.vector.memset(planes[h][:].bitcast(I32), 0)
+        nc.vector.memset(planes[1][:].bitcast(I32), 0)
         ident_f = keep.tile([P, P], F32, name="ident_f")
         ident_b = keep.tile([P, P], BF16, name="ident_b")
-        make_identity(nc, ident_f[:])
-        for h in range(2):
+
+        def load_planes(h):
             for q in range(4):
                 nc.gpsimd.dma_start(
                     out=planes[h][32 * q : 32 * q + 16, :].bitcast(F32),
                     in_=w_scales[4 * h : 4 * h + 4, 4 * q : 4 * q + 4, :].bitcast(F32),
                 )
+
         make_identity(nc, ident_b[:])
+        load_planes(0)
+        make_identity(nc, ident_f[:])
+        load_planes(1)
 
         x_sb = []
         for t in range(4):
@@ -66,6 +70,20 @@ def tile_vdl_w_kernel(tc, x, w_words, w_scales, b, out):
                     in_=w_words[g].rearrange("p n t -> p (n t)")[:, 4 * c0 : 4 * c1].bitcast(I32),
                 )
                 w_sb[(bi, g)] = wt
+
+        spread = []
+        for i in range(4):
+            bp = psum.tile([P, 2 * BANK], BF16, name="bp%d" % i, tag="bank%d" % (4 + i))
+            for e in range(2):
+                j = 2 * i + e
+                nc.tensor.matmul(
+                    out=bp[:, BANK * e : BANK * (e + 1)],
+                    lhsT=ident_b[:, j : j + 1].to_broadcast([P, P]),
+                    rhs=bias_rows[:],
+                    start=True,
+                    stop=True,
+                )
+            spread.append(bp)
 
         x_codes = []
         x_scales = []
@@ -91,27 +109,12 @@ def tile_vdl_w_kernel(tc, x, w_words, w_scales, b, out):
             x_codes.append(xc)
             x_scales.append(xs)
 
-        bias_p = keep.tile([P, 4, N_OUT // 4], F32, name="bias_p")
-
-        def bias_round(js, banks):
-            spread = []
-            for j, bank in zip(js, banks):
-                bp = psum.tile([P, BANK], F32, name="bp%d" % j, tag="bank%d" % bank)
-                nc.tensor.matmul(
-                    out=bp[:],
-                    lhsT=ident_b[:, j : j + 1].to_broadcast([P, P]),
-                    rhs=bias_rows[:],
-                    start=True,
-                    stop=True,
-                )
-                spread.append(bp)
-            for i, j in enumerate(js):
-                dst = bias_p[:, :, (BANK // 4) * j : (BANK // 4) * (j + 1)]
-                src = spread[i][:].rearrange("p (c a) -> p a c", a=4)
-                if i % 2 == 0:
-                    nc.scalar.copy(out=dst, in_=src)
-                else:
-                    nc.vector.tensor_copy(out=dst, in_=src)
+        bias_p = keep.tile([P, 4, N_OUT // 4], BF16, name="bias_p")
+        for i in range(4):
+            nc.scalar.copy(
+                out=bias_p[:, :, (BANK // 2) * i : (BANK // 2) * (i + 1)],
+                in_=spread[i][:].rearrange("p (c a) -> p a c", a=4),
+            )
 
         pieces = []
         n_pieces = 0
@@ -167,13 +170,7 @@ def tile_vdl_w_kernel(tc, x, w_words, w_scales, b, out):
             nc.vector.tensor_copy(out=res[:].rearrange("p (c a) -> p c a", a=4), in_=y[:].rearrange("p a c -> p c a"))
             nc.sync.dma_start(out=out[:, c0:c1], in_=res[:])
 
-        bias_round((0, 1, 2, 3), (4, 5, 6, 7))
-        passes(0, 0)
-        bias_round((4, 5, 6, 7), (4, 5, 6, 7))
-        for g in range(1, GROUPS):
-            passes(0, g)
-        epilogue(0)
-        for bi in range(1, len(BATCHES)):
+        for bi in range(len(BATCHES)):
             for g in range(GROUPS):
                 passes(bi, g)
             epilogue(bi)

@@ -21,6 +21,7 @@ BANK = 512
 BANKS = 8
 N_OUT = 4096
 BATCHES = ((0, 2048), (2048, 3328), (3328, 3840), (3840, 4096))
+RUNS = (((0, 1), (1, 2), (2, 3), (3, 4), (4, 5), (5, 6), (6, 7), (7, 8)), ((0, 1), (1, 2), (2, 3), (3, 4), (4, 5), (5, 6), (6, 7), (7, 8)), ((0, 2), (2, 4), (4, 6), (6, 7), (7, 8)), ((0, 4), (4, 6), (6, 7), (7, 8)))
 TANH, SIN, RELU, SIGMOID = 0, 1, 2, 3
 TWO_PI = 2.0 * math.pi
 
@@ -63,13 +64,14 @@ def tile_vdl_w_kernel(tc, x, w_words, w_scales, b, out):
             x_sb.append(xs_t)
         w_sb = {}
         for bi, (c0, c1) in enumerate(BATCHES):
-            for g in range(GROUPS):
-                wt = keep.tile([P, c1 - c0], U32, name="w%d_%d" % (bi, g), align_bytes=64)
+            for g0, g1 in RUNS[bi]:
+                wt = keep.tile([P, g1 - g0, c1 - c0], U32, name="w%d_%d" % (bi, g0), align_bytes=64)
                 nc.sync.dma_start(
                     out=wt[:].bitcast(I32),
-                    in_=w_words[g].rearrange("p n t -> p (n t)")[:, 4 * c0 : 4 * c1].bitcast(I32),
+                    in_=w_words[g0:g1].rearrange("g p n t -> p g (n t)")[:, :, 4 * c0 : 4 * c1].bitcast(I32),
                 )
-                w_sb[(bi, g)] = wt
+                for g in range(g0, g1):
+                    w_sb[(bi, g)] = wt[:, g - g0, :]
 
         spread = []
         for i in range(4):

import math
from contextlib import ExitStack

import concourse.mybir as mybir
from concourse.masks import make_identity

FLOPS = 2 * 128 * 4096 * 4096

F32 = mybir.dt.float32
BF16 = mybir.dt.bfloat16
I32 = mybir.dt.int32
U32 = mybir.dt.uint32
U8 = mybir.dt.uint8
FP8X4 = mybir.dt.float8_e4m3fn_x4
ALU = mybir.AluOpType
ACT = mybir.ActivationFunctionType

P = 128
GROUPS = 8
BANK = 512
BANKS = 8
N_OUT = 4096
BATCHES = ((0, 2048), (2048, 3328), (3328, 3840), (3840, 4096))
RUNS = (((0, 1), (1, 2), (2, 3), (3, 4), (4, 5), (5, 6), (6, 7), (7, 8)), ((0, 1), (1, 2), (2, 3), (3, 4), (4, 5), (5, 6), (6, 7), (7, 8)), ((0, 2), (2, 4), (4, 6), (6, 7), (7, 8)), ((0, 4), (4, 6), (6, 7), (7, 8)))
TANH, SIN, RELU, SIGMOID = 0, 1, 2, 3
TWO_PI = 2.0 * math.pi


def tile_vdl_w_kernel(tc, x, w_words, w_scales, b, out):
    nc = tc.nc
    with ExitStack() as ctx:
        keep = ctx.enter_context(tc.tile_pool(name="keep", bufs=1))
        psum = ctx.enter_context(tc.psum_pool(name="psum", bufs=1))
        ctx.enter_context(tc.manual_schedule())

        planes = [keep.tile([P, N_OUT], U8, name="plane%d" % h, align_bytes=64) for h in range(2)]
        bias_rows = keep.tile([P, BANK], BF16, name="bias_rows")
        nc.vector.memset(bias_rows[:].bitcast(I32), 0)
        nc.scalar.dma_start(out=bias_rows[0:8, :], in_=b.rearrange("(j n) -> j n", j=8))
        nc.vector.memset(planes[0][:].bitcast(I32), 0)
        warm = keep.tile([P, 2], F32, name="warm")
        nc.vector.memset(warm[:, 0:1], 0.0)
        nc.scalar.activation(out=warm[:, 1:2], in_=warm[:, 0:1], func=ACT.Silu)
        nc.vector.memset(planes[1][:].bitcast(I32), 0)
        ident_f = keep.tile([P, P], F32, name="ident_f")
        ident_b = keep.tile([P, P], BF16, name="ident_b")

        def load_planes(h):
            for q in range(4):
                nc.gpsimd.dma_start(
                    out=planes[h][32 * q : 32 * q + 16, :].bitcast(F32),
                    in_=w_scales[4 * h : 4 * h + 4, 4 * q : 4 * q + 4, :].bitcast(F32),
                )

        make_identity(nc, ident_b[:])
        load_planes(0)
        make_identity(nc, ident_f[:])
        load_planes(1)

        x_sb = []
        for t in range(4):
            xs_t = keep.tile([P, 1024], BF16, name="x_sb%d" % t)
            nc.sync.dma_start(out=xs_t[:], in_=x[:, 1024 * t : 1024 * (t + 1)])
            x_sb.append(xs_t)
        w_sb = {}
        for bi, (c0, c1) in enumerate(BATCHES):
            for g0, g1 in RUNS[bi]:
                wt = keep.tile([P, g1 - g0, c1 - c0], U32, name="w%d_%d" % (bi, g0), align_bytes=64)
                nc.sync.dma_start(
                    out=wt[:].bitcast(I32),
                    in_=w_words[g0:g1].rearrange("g p n t -> p g (n t)")[:, :, 4 * c0 : 4 * c1].bitcast(I32),
                )
                for g in range(g0, g1):
                    w_sb[(bi, g)] = wt[:, g - g0, :]

        spread = []
        for i in range(4):
            bp = psum.tile([P, 2 * BANK], BF16, name="bp%d" % i, tag="bank%d" % (4 + i))
            for e in range(2):
                j = 2 * i + e
                nc.tensor.matmul(
                    out=bp[:, BANK * e : BANK * (e + 1)],
                    lhsT=ident_b[:, j : j + 1].to_broadcast([P, P]),
                    rhs=bias_rows[:],
                    start=True,
                    stop=True,
                )
            spread.append(bp)

        x_codes = []
        x_scales = []
        for t in range(4):
            x_words = x_sb[t][:].bitcast(F32)
            xt = psum.tile([P, 2, 2, P], F32, name="xt%d" % t, tag="bank%d" % t)
            for gi in range(2):
                for u in range(2):
                    nc.tensor.transpose(xt[:, gi, u, :], x_words[:, 256 * gi + u : 256 * (gi + 1) : 2], ident_f[:])
            gt = keep.tile([P, 2, P, 4], BF16, name="grouped%d" % t, align_bytes=64)
            src = xt[:].rearrange("p g u r -> p g r u")
            if t % 2 == 0:
                nc.vector.tensor_copy(out=gt[:].bitcast(F32), in_=src)
            else:
                nc.scalar.copy(out=gt[:].bitcast(F32), in_=src)
            xc = keep.tile([P, 2 * P], U32, name="x_codes%d" % t, align_bytes=64)
            xs = keep.tile([P, 2 * P], U8, name="x_scales%d" % t, align_bytes=64)
            nc.vector.quantize_mx(
                out=xc[:].bitcast(FP8X4),
                scales=xs[:],
                in_=gt[:].rearrange("p g r t -> p (g r t)"),
            )
            x_codes.append(xc)
            x_scales.append(xs)

        bias_p = keep.tile([P, 4, N_OUT // 4], BF16, name="bias_p")
        for i in range(4):
            nc.scalar.copy(
                out=bias_p[:, :, (BANK // 2) * i : (BANK // 2) * (i + 1)],
                in_=spread[i][:].rearrange("p (c a) -> p a c", a=4),
            )

        pieces = []
        n_pieces = 0
        for c0, c1 in BATCHES:
            row = []
            for c in range(c0, c1, BANK):
                row.append((c, min(BANK, c1 - c), n_pieces % BANKS))
                n_pieces += 1
            pieces.append(row)
        acc = {}

        def passes(bi, g):
            c0 = BATCHES[bi][0]
            for c, n, bank in pieces[bi]:
                if g == 0:
                    acc[c] = psum.tile([P, n], F32, name="acc%d" % c, tag="bank%d" % bank)
                k = 4 * (g % 4)
                nc.tensor.matmul_mx(
                    out=acc[c][:],
                    lhsT=x_codes[g // 2][:, P * (g % 2) : P * (g % 2 + 1)].bitcast(FP8X4),
                    lhsT_scale=x_scales[g // 2][:, P * (g % 2) : P * (g % 2 + 1)],
                    rhs=w_sb[(bi, g)][:, c - c0 : c - c0 + n].bitcast(FP8X4),
                    rhs_scale=planes[g // 4][k:P, c : c + n],
                    start=(g == 0),
                    stop=(g == GROUPS - 1),
                )

        def epilogue(bi):
            c0, c1 = BATCHES[bi]
            width = (c1 - c0) // 4
            y = keep.tile([P, 4, width], F32, name="y%d" % bi)
            turns = keep.tile([P, width], I32, name="turns%d" % bi)
            res = keep.tile([P, 4 * width], F32, name="res%d" % bi)
            for half in (slice(0, 2), slice(2, 4)):
                for c, n, bank in pieces[bi]:
                    nc.vector.tensor_tensor(
                        out=y[:, half, (c - c0) // 4 : (c - c0 + n) // 4],
                        in0=acc[c][:].rearrange("p (c a) -> p a c", a=4)[:, half, :],
                        in1=bias_p[:, half, c // 4 : (c + n) // 4],
                        op=ALU.add,
                    )
            nc.scalar.activation(out=y[:, TANH, :], in_=y[:, TANH, :], func=ACT.Tanh)
            nc.scalar.activation(out=y[:, SIGMOID, :], in_=y[:, SIGMOID, :], func=ACT.Tanh, scale=0.5)
            nc.vector.tensor_scalar(out=turns[:], in0=y[:, SIN, :], scalar1=1.0 / TWO_PI, scalar2=None, op0=ALU.mult)
            nc.vector.tensor_scalar_max(out=y[:, RELU, :], in0=y[:, RELU, :], scalar1=0.0)
            nc.vector.scalar_tensor_tensor(
                out=y[:, SIN, :], in0=turns[:], scalar=-TWO_PI, in1=y[:, SIN, :], op0=ALU.mult, op1=ALU.add
            )
            nc.scalar.activation(out=y[:, SIN, :], in_=y[:, SIN, :], func=ACT.Sin)
            nc.vector.tensor_scalar(
                out=y[:, SIGMOID, :], in0=y[:, SIGMOID, :], scalar1=0.5, scalar2=0.5, op0=ALU.mult, op1=ALU.add
            )
            nc.vector.tensor_copy(out=res[:].rearrange("p (c a) -> p c a", a=4), in_=y[:].rearrange("p a c -> p c a"))
            nc.sync.dma_start(out=out[:, c0:c1], in_=res[:])

        for bi in range(len(BATCHES)):
            for g in range(GROUPS):
                passes(bi, g)
            epilogue(bi)
